import numpy as np
import ml_dtypes


def mxq(x, axis, fmt="e4m3"):
    dtype, down = {"e4m3": (ml_dtypes.float8_e4m3fn, 7), "e5m2": (ml_dtypes.float8_e5m2, 14)}[fmt]
    v = np.moveaxis(np.asarray(x, np.float32).astype(ml_dtypes.bfloat16).astype(np.float64), axis, -1)
    blocks = v.reshape(v.shape[:-1] + (-1, 32))
    amax = np.abs(blocks).max(-1, keepdims=True)
    byte = np.maximum(np.where(amax > 0, np.frexp(amax)[1] - 1 + 127, 0) - down, 1)
    scale = np.exp2(byte - 127.0)
    codes = (blocks / scale).astype(np.float32).astype(dtype).astype(np.float64)
    return np.moveaxis((codes * scale).reshape(v.shape), -1, axis)


WIDE = False


def mx_kscale(k):
    if not WIDE:
        return np.ones(k)
    levels = np.array([10, -10, 5, -5, 0])
    a = np.random.permutation(np.resize(levels, k // 512 * 4)).reshape(k // 512, 4)
    idx = np.arange(k)
    return np.exp2(a[idx // 512, idx % 128 // 32])


BF16 = ml_dtypes.bfloat16


def bf(x):
    return np.asarray(x, np.float32).astype(BF16)


def f64(x):
    return np.asarray(x).astype(np.float64)


B, T, C, NH, HS, NLQ, NLKV, DHR = 4, 1024, 512, 2, 256, 512, 512, 128
THETA = 10000.0


def rope(v, cos, sin):
    vr = v.reshape(v.shape[:-1] + (-1, 2))
    re, im = vr[..., 0], vr[..., 1]
    c = cos[None, :, None, :]
    s = sin[None, :, None, :]
    return np.stack([re * c - im * s, re * s + im * c], axis=-1).reshape(v.shape)


def setup_inputs():
    s, t = mx_kscale(C), mx_kscale(NLQ)
    ang = np.outer(np.arange(T), 1.0 / THETA ** (np.arange(0, DHR, 2) / DHR))
    return {"x": bf(np.random.standard_normal((B, T, C)) * s),
            "cos": bf(np.cos(ang)),
            "sin": bf(np.sin(ang)),
            "W_dq": bf(np.random.standard_normal((NLQ, C)) / np.sqrt(C) / s[None, :] * t[:, None]),
            "W_uq": bf((np.random.standard_normal((NLQ, C)) / np.sqrt(NLQ) / t[:, None]).reshape(C, NLQ)),
            "W_uk": bf(np.random.standard_normal((C, NLKV)) / np.sqrt(HS)),
            "W_qr": bf(np.random.standard_normal((NH * DHR, NLQ)) / np.sqrt(NLQ) / t[None, :])}


def reference(x, cos, sin, W_dq, W_uq, W_uk, W_qr):
    cq = mxq(mxq(f64(x), 2, "e4m3") @ mxq(f64(W_dq), 1, "e4m3").T, 2, "e4m3")
    k_eff = f64(W_uq).reshape(NLQ, NH, HS).transpose(1, 0, 2) @ f64(W_uk).reshape(NH, HS, NLKV)
    q_abs = cq[:, None] @ mxq(k_eff, 1, "e4m3")[None]
    c_qr = (cq @ mxq(f64(W_qr), 1, "e4m3").T).reshape(B, T, NH, DHR)
    return q_abs, rope(c_qr, f64(cos), f64(sin))

@@ -1,0 +1,274 @@
+from contextlib import ExitStack
+
+import concourse.mybir as mybir
+from concourse.masks import make_identity
+
+F32 = mybir.dt.float32
+BF16 = mybir.dt.bfloat16
+U32 = mybir.dt.uint32
+U8 = mybir.dt.uint8
+FP8X4 = mybir.dt.float8_e4m3fn_x4
+MULT = mybir.AluOpType.mult
+ADD = mybir.AluOpType.add
+
+B, T, C = 4, 1024, 512
+NH, HS = 2, 256
+NLQ, NLKV, DHR = 512, 512, 128
+
+P = 128
+PACK = 4
+WORDS = 2
+ROT = NH * DHR
+TILES_PER_BATCH = T // P
+PAIR = 2
+GROUP = 4
+N_PAIRS = B * TILES_PER_BATCH // PAIR
+N_GROUPS = B * TILES_PER_BATCH // GROUP
+GROUPS_PER_BATCH = TILES_PER_BATCH // GROUP
+
+FLOPS = 2 * B * T * NLQ * (C + NH * NLKV + ROT) + 2 * NH * NLQ * HS * NLKV
+
+
+def quantise(nc, grouped, operand):
+    codes, scales = operand
+    nc.vector.quantize_mx(
+        out=codes.bitcast(FP8X4), scales=scales, in_=grouped.rearrange("p c t -> p (c t)")
+    )
+
+
+def columns(operand, first, count):
+    codes, scales = operand
+    return codes[:, first : first + count], scales[:, first : first + count]
+
+
+def mx_pass(nc, out, stationary, moving):
+    nc.tensor.matmul_mx(
+        out=out,
+        lhsT=stationary[0].bitcast(FP8X4),
+        lhsT_scale=stationary[1],
+        rhs=moving[0].bitcast(FP8X4),
+        rhs_scale=moving[1],
+        start=True,
+        stop=True,
+    )
+
+
+def tile_causalselfattention_pa_t_kernel(tc, x, cos, sin, W_dq, W_uq, W_uk, W_qr, out_0, out_1):
+    nc = tc.nc
+    with ExitStack() as ctx:
+        ctx.enter_context(tc.manual_schedule())
+        const = ctx.enter_context(tc.tile_pool(name="const", bufs=1))
+        grouped_pool = ctx.enter_context(tc.tile_pool(name="grouped", bufs=2))
+        mx_pool = ctx.enter_context(tc.tile_pool(name="mx", bufs=3))
+        rope_pool = ctx.enter_context(tc.tile_pool(name="rope", bufs=2))
+        rows_pool = ctx.enter_context(tc.tile_pool(name="rows", bufs=3))
+        tr_banks = ctx.enter_context(tc.psum_pool(name="tr_banks", bufs=1))
+        cq_banks = ctx.enter_context(tc.psum_pool(name="cq_banks", bufs=2))
+        qa_banks = ctx.enter_context(tc.psum_pool(name="qa_banks", bufs=4))
+        qr_banks = ctx.enter_context(tc.psum_pool(name="qr_banks", bufs=1))
+
+        def mx_tiles(pool, width, name):
+            codes = pool.tile([P, width], U32, name=name + "_codes", tag=name + "_codes", align_bytes=64)
+            scales = pool.tile([P, width], U8, name=name + "_scales", tag=name + "_scales", align_bytes=64)
+            return codes[:], scales[:]
+
+        x_view = x.rearrange("b (p a) k -> b p a k", a=TILES_PER_BATCH)
+        x_words = []
+
+        def load_x(group):
+            b, part = divmod(group, GROUPS_PER_BATCH)
+            x_rows = const.tile([P, GROUP, C], BF16, name="x_rows%d" % group)
+            nc.sync.dma_start(out=x_rows[:], in_=x_view[b, :, part * GROUP : (part + 1) * GROUP, :])
+            x_words.append(x_rows[:].bitcast(F32))
+
+        wdq_rows = const.tile([P, PACK, C], BF16)
+        nc.sync.dma_start(out=wdq_rows[:], in_=W_dq.rearrange("(m j) k -> m j k", j=PACK))
+        load_x(0)
+        wuq_rows = const.tile([P, PACK, NH * HS], BF16)
+        nc.sync.dma_start(out=wuq_rows[:], in_=W_uq.rearrange("(m j) c -> m j c", j=PACK))
+        wuk_rows = const.tile([P, NH, WORDS, NLKV], BF16)
+        nc.sync.dma_start(out=wuk_rows[:], in_=W_uk.rearrange("(h q e) n -> q h e n", h=NH, e=WORDS))
+        wqr_rows = const.tile([P, 2, NLQ], BF16)
+        nc.sync.dma_start(out=wqr_rows[:], in_=W_qr.rearrange("(m e) l -> m e l", e=2))
+        cos_rows = const.tile([P, TILES_PER_BATCH, DHR // 2], BF16)
+        nc.sync.dma_start(out=cos_rows[:], in_=cos.rearrange("(p a) i -> p a i", a=TILES_PER_BATCH))
+        sin_rows = const.tile([P, TILES_PER_BATCH, DHR // 2], BF16)
+        nc.sync.dma_start(out=sin_rows[:], in_=sin.rearrange("(p a) i -> p a i", a=TILES_PER_BATCH))
+        for group in range(1, N_GROUPS):
+            load_x(group)
+
+        identity = const.tile([P, P], F32)
+        make_identity(nc, identity[:])
+
+        def rope_table(rows, sign, name):
+            table = const.tile([P, TILES_PER_BATCH, NH, DHR // 2], F32, name=name)
+            nc.gpsimd.tensor_scalar(
+                out=table[:],
+                in0=rows[:].unsqueeze(2).to_broadcast([P, TILES_PER_BATCH, NH, DHR // 2]),
+                scalar1=sign,
+                scalar2=0.0,
+                op0=MULT,
+                op1=ADD,
+            )
+            return table[:].rearrange("p a h i -> p a (h i)")
+
+        cos_table = rope_table(cos_rows, 1.0, "cos_table")
+        sin_table = rope_table(sin_rows, 1.0, "sin_table")
+        minus_sin_table = rope_table(sin_rows, -1.0, "minus_sin_table")
+
+        def transpose_two_tiles(bank, tiles_of_words):
+            for s, words in enumerate(tiles_of_words):
+                for u in range(WORDS):
+                    nc.tensor.transpose(bank[:, u, s * P : (s + 1) * P], words[:, u * P : (u + 1) * P], identity[:])
+
+        def regroup_words(copy, grouped, bank):
+            copy(out=grouped.bitcast(F32), in_=bank[:].rearrange("p u c -> p c u"))
+
+        wdq_words = wdq_rows[:].bitcast(F32)
+        wdq_grouped = const.tile([P, NLQ, PACK], BF16, align_bytes=64)
+        wdq_mx = mx_tiles(const, NLQ, "wdq")
+        for half, copy in enumerate((nc.scalar.copy, nc.vector.tensor_copy)):
+            bank = qa_banks.tile([P, WORDS, PAIR * P], F32, tag="bank")
+            transpose_two_tiles(bank, [wdq_words[:, PAIR * half + s, :] for s in range(PAIR)])
+            regroup_words(copy, wdq_grouped[:, PAIR * P * half : PAIR * P * (half + 1), :], bank)
+        quantise(nc, wdq_grouped[:], wdq_mx)
+
+        x_mx = {}
+        cq_mx = {}
+        x_grouped = {}
+        cq_grouped = {}
+
+        def transpose_x(pair):
+            group, first = divmod(pair * PAIR, GROUP)
+            bank = tr_banks.tile([P, WORDS, PAIR * P], F32, tag="bank")
+            transpose_two_tiles(bank, [x_words[group][:, first + s, :] for s in range(PAIR)])
+            grouped = grouped_pool.tile([P, PAIR * P, PACK], BF16, tag="x", align_bytes=64)
+            regroup_words(nc.scalar.copy, grouped[:], bank)
+            x_grouped[pair] = grouped
+
+        def quantise_x(pair):
+            x_mx[pair] = mx_tiles(mx_pool, PAIR * P, "x")
+            quantise(nc, x_grouped[pair][:], x_mx[pair])
+
+        def project_cq(pair):
+            grouped = grouped_pool.tile([P, PAIR * P, PACK], BF16, tag="cq", align_bytes=64)
+            for s in range(PAIR):
+                bank = cq_banks.tile([P, PACK, P], F32, tag="bank")
+                for j in range(PACK):
+                    mx_pass(nc, bank[:, j, :], columns(wdq_mx, j * P, P), columns(x_mx[pair], s * P, P))
+                nc.vector.tensor_copy(
+                    out=grouped[:, s * P : (s + 1) * P, :], in_=bank[:].rearrange("p j t -> p t j")
+                )
+            cq_grouped[pair] = grouped
+
+        def quantise_cq(pair):
+            cq_mx[pair] = mx_tiles(mx_pool, PAIR * P, "cq")
+            quantise(nc, cq_grouped[pair][:], cq_mx[pair])
+
+        transpose_x(0)
+        quantise_x(0)
+
+        wuq_words = wuq_rows[:].bitcast(F32)
+        wuq_t = []
+        for h, copy in enumerate((nc.scalar.copy, nc.vector.tensor_copy)):
+            bank = qa_banks.tile([P, PACK, P], F32, tag="bank")
+            for j in range(PACK):
+                nc.tensor.transpose(bank[:, j, :], wuq_words[:, j, h * P : (h + 1) * P], identity[:])
+            transposed = const.tile([P, PACK * P], F32, name="wuq_t%d" % h)
+            copy(out=transposed[:], in_=bank[:].rearrange("p j m -> p (j m)"))
+            wuq_t.append(transposed[:].bitcast(BF16).rearrange("p (c e) -> p c e", e=WORDS))
+
+        project_cq(0)
+
+        keff_grouped = const.tile([P, NH * NLKV, PACK], BF16, align_bytes=64)
+        keff_mx = mx_tiles(const, NH * NLKV, "keff")
+        for h in range(NH):
+            for n_block in range(NLKV // P):
+                bank = qa_banks.tile([P, PACK, P], F32, tag="bank")
+                for j in range(PACK):
+                    for e in range(WORDS):
+                        nc.tensor.matmul(
+                            out=bank[:, j, :],
+                            lhsT=wuq_t[h][:, j * P : (j + 1) * P, e],
+                            rhs=wuk_rows[:, h, e, n_block * P : (n_block + 1) * P],
+                            start=(e == 0),
+                            stop=(e == WORDS - 1),
+                        )
+                copy = nc.scalar.copy if n_block % 2 == 0 else nc.vector.tensor_copy
+                first = h * NLKV + n_block * P
+                copy(out=keff_grouped[:, first : first + P, :], in_=bank[:].rearrange("p j n -> p n j"))
+            if h == 0:
+                quantise_cq(0)
+            quantise(nc, keff_grouped[:, h * NLKV : (h + 1) * NLKV, :], columns(keff_mx, h * NLKV, NLKV))
+
+        wqr_words = wqr_rows[:].bitcast(F32).rearrange("m e (p u) -> m e u p", u=WORDS)
+        wqr_grouped = const.tile([P, ROT, PACK], BF16, align_bytes=64)
+        wqr_mx = mx_tiles(const, ROT, "wqr")
+        bank = qr_banks.tile([P, WORDS, ROT], F32, tag="bank")
+        for e in range(2):
+            for u in range(WORDS):
+                nc.tensor.transpose(bank[:, u, e * P : (e + 1) * P], wqr_words[:, e, u, :], identity[:])
+        regroup_words(nc.scalar.copy, wqr_grouped[:], bank)
+        transpose_x(1)
+        quantise(nc, wqr_grouped[:], wqr_mx)
+        quantise_x(1)
+
+        q_abs_view = out_0.rearrange("b h (p a) n -> b h p a n", a=TILES_PER_BATCH)
+        q_r_view = out_1.rearrange("b (p a) h d -> b p a (h d)", a=TILES_PER_BATCH)
+        q_abs_rows = []
+        q_r_rows = []
+        for pair in range(N_PAIRS):
+            group, first = divmod(pair * PAIR, GROUP)
+            b, part = divmod(group, GROUPS_PER_BATCH)
+            a = part * GROUP + first
+            if first == 0:
+                q_abs_rows = [
+                    rows_pool.tile([P, GROUP, NLKV], F32, name="q_abs_rows%d" % h, tag="q_abs%d" % h)
+                    for h in range(NH)
+                ]
+                q_r_rows = rows_pool.tile([P, GROUP, ROT], F32, tag="q_r")
+            last_of_group = first + PAIR == GROUP
+            group_tiles = slice(part * GROUP, (part + 1) * GROUP)
+
+            if pair + 2 < N_PAIRS:
+                transpose_x(pair + 2)
+            if pair + 1 < N_PAIRS:
+                project_cq(pair + 1)
+
+            rot_bank = qr_banks.tile([P, PAIR, 2, P], F32, tag="bank")
+            for s in range(PAIR):
+                mx_pass(nc, rot_bank[:, s, :, :].rearrange("p e m -> p (e m)"), columns(cq_mx[pair], s * P, P), wqr_mx)
+            by_cos = rope_pool.tile([P, PAIR, 2, P], F32, tag="by_cos")
+            nc.vector.tensor_tensor(
+                out=by_cos[:],
+                in0=rot_bank[:],
+                in1=cos_table[:, a : a + PAIR, :].unsqueeze(2).to_broadcast([P, PAIR, 2, P]),
+                op=MULT,
+            )
+            if pair + 2 < N_PAIRS:
+                quantise_x(pair + 2)
+            if pair + 1 < N_PAIRS:
+                quantise_cq(pair + 1)
+            by_sin = rope_pool.tile([P, PAIR, 2, P], F32, tag="by_sin")
+            nc.vector.tensor_tensor(
+                out=by_sin[:, :, 0, :], in0=rot_bank[:, :, 1, :], in1=minus_sin_table[:, a : a + PAIR, :], op=MULT
+            )
+            nc.vector.tensor_tensor(
+                out=by_sin[:, :, 1, :], in0=rot_bank[:, :, 0, :], in1=sin_table[:, a : a + PAIR, :], op=MULT
+            )
+            nc.gpsimd.tensor_tensor(
+                out=q_r_rows[:, first : first + PAIR, :].rearrange("p s (m e) -> p s m e", e=2),
+                in0=by_cos[:].rearrange("p s e m -> p s m e"),
+                in1=by_sin[:].rearrange("p s e m -> p s m e"),
+                op=ADD,
+            )
+
+            for h in range(NH):
+                for s in range(PAIR):
+                    acc = qa_banks.tile([P, NLKV], F32, tag="bank")
+                    mx_pass(nc, acc[:], columns(cq_mx[pair], s * P, P), columns(keff_mx, h * NLKV, NLKV))
+                    nc.scalar.copy(out=q_abs_rows[h][:, first + s, :], in_=acc[:])
+                if last_of_group:
+                    nc.sync.dma_start(out=q_abs_view[b, h, :, group_tiles, :], in_=q_abs_rows[h][:])
+                    if h == 0:
+                        nc.sync.dma_start(out=q_r_view[b, :, group_tiles, :], in_=q_r_rows[:])

@@ -61,7 +61,7 @@ def tile_causalselfattention_pa_t_kernel(tc, x, cos, sin, W_dq, W_uq, W_uk, W_qr
         grouped_pool = ctx.enter_context(tc.tile_pool(name="grouped", bufs=2))
         mx_pool = ctx.enter_context(tc.tile_pool(name="mx", bufs=3))
         rope_pool = ctx.enter_context(tc.tile_pool(name="rope", bufs=2))
-        rows_pool = ctx.enter_context(tc.tile_pool(name="rows", bufs=3))
+        rows_pool = ctx.enter_context(tc.tile_pool(name="rows", bufs=6))
         tr_banks = ctx.enter_context(tc.psum_pool(name="tr_banks", bufs=1))
         cq_banks = ctx.enter_context(tc.psum_pool(name="cq_banks", bufs=2))
         qa_banks = ctx.enter_context(tc.psum_pool(name="qa_banks", bufs=4))
@@ -100,21 +100,16 @@ def tile_causalselfattention_pa_t_kernel(tc, x, cos, sin, W_dq, W_uq, W_uk, W_qr
         identity = const.tile([P, P], F32)
         make_identity(nc, identity[:])
 
-        def rope_table(rows, sign, name):
-            table = const.tile([P, TILES_PER_BATCH, NH, DHR // 2], F32, name=name)
+        rotation = const.tile([P, TILES_PER_BATCH, 2, 2, P], F32)
+        for f, e, rows, sign in ((0, 0, cos_rows, 1.0), (0, 1, sin_rows, -1.0), (1, 0, sin_rows, 1.0), (1, 1, cos_rows, 1.0)):
             nc.gpsimd.tensor_scalar(
-                out=table[:],
+                out=rotation[:, :, f, e, :].rearrange("p a (h i) -> p a h i", h=NH),
                 in0=rows[:].unsqueeze(2).to_broadcast([P, TILES_PER_BATCH, NH, DHR // 2]),
                 scalar1=sign,
                 scalar2=0.0,
                 op0=MULT,
                 op1=ADD,
             )
-            return table[:].rearrange("p a h i -> p a (h i)")
-
-        cos_table = rope_table(cos_rows, 1.0, "cos_table")
-        sin_table = rope_table(sin_rows, 1.0, "sin_table")
-        minus_sin_table = rope_table(sin_rows, -1.0, "minus_sin_table")
 
         def transpose_two_tiles(bank, tiles_of_words):
             for s, words in enumerate(tiles_of_words):
@@ -178,7 +173,20 @@ def tile_causalselfattention_pa_t_kernel(tc, x, cos, sin, W_dq, W_uq, W_uk, W_qr
             copy(out=transposed[:], in_=bank[:].rearrange("p j m -> p (j m)"))
             wuq_t.append(transposed[:].bitcast(BF16).rearrange("p (c e) -> p c e", e=WORDS))
 
+        transpose_x(1)
+        quantise_x(1)
         project_cq(0)
+
+        wqr_words = wqr_rows[:].bitcast(F32).rearrange("m e (p u) -> m e u p", u=WORDS)
+        wqr_grouped = const.tile([P, ROT, PACK], BF16, align_bytes=64)
+        wqr_mx = mx_tiles(const, ROT, "wqr")
+        bank = qr_banks.tile([P, WORDS, ROT], F32, tag="bank")
+        for e in range(2):
+            for u in range(WORDS):
+                nc.tensor.transpose(bank[:, u, e * P : (e + 1) * P], wqr_words[:, e, u, :], identity[:])
+        regroup_words(nc.scalar.copy, wqr_grouped[:], bank)
+        quantise_cq(0)
+        quantise(nc, wqr_grouped[:], wqr_mx)
 
         keff_grouped = const.tile([P, NH * NLKV, PACK], BF16, align_bytes=64)
         keff_mx = mx_tiles(const, NH * NLKV, "keff")
@@ -197,78 +205,48 @@ def tile_causalselfattention_pa_t_kernel(tc, x, cos, sin, W_dq, W_uq, W_uk, W_qr
                 copy = nc.scalar.copy if n_block % 2 == 0 else nc.vector.tensor_copy
                 first = h * NLKV + n_block * P
                 copy(out=keff_grouped[:, first : first + P, :], in_=bank[:].rearrange("p j n -> p n j"))
-            if h == 0:
-                quantise_cq(0)
             quantise(nc, keff_grouped[:, h * NLKV : (h + 1) * NLKV, :], columns(keff_mx, h * NLKV, NLKV))
-
-        wqr_words = wqr_rows[:].bitcast(F32).rearrange("m e (p u) -> m e u p", u=WORDS)
-        wqr_grouped = const.tile([P, ROT, PACK], BF16, align_bytes=64)
-        wqr_mx = mx_tiles(const, ROT, "wqr")
-        bank = qr_banks.tile([P, WORDS, ROT], F32, tag="bank")
-        for e in range(2):
-            for u in range(WORDS):
-                nc.tensor.transpose(bank[:, u, e * P : (e + 1) * P], wqr_words[:, e, u, :], identity[:])
-        regroup_words(nc.scalar.copy, wqr_grouped[:], bank)
-        transpose_x(1)
-        quantise(nc, wqr_grouped[:], wqr_mx)
-        quantise_x(1)
 
         q_abs_view = out_0.rearrange("b h (p a) n -> b h p a n", a=TILES_PER_BATCH)
         q_r_view = out_1.rearrange("b (p a) h d -> b p a (h d)", a=TILES_PER_BATCH)
-        q_abs_rows = []
-        q_r_rows = []
         for pair in range(N_PAIRS):
-            group, first = divmod(pair * PAIR, GROUP)
-            b, part = divmod(group, GROUPS_PER_BATCH)
-            a = part * GROUP + first
-            if first == 0:
-                q_abs_rows = [
-                    rows_pool.tile([P, GROUP, NLKV], F32, name="q_abs_rows%d" % h, tag="q_abs%d" % h)
-                    for h in range(NH)
-                ]
-                q_r_rows = rows_pool.tile([P, GROUP, ROT], F32, tag="q_r")
-            last_of_group = first + PAIR == GROUP
-            group_tiles = slice(part * GROUP, (part + 1) * GROUP)
+            b, a = divmod(pair * PAIR, TILES_PER_BATCH)
+            last = pair == N_PAIRS - 1
 
             if pair + 2 < N_PAIRS:
                 transpose_x(pair + 2)
             if pair + 1 < N_PAIRS:
                 project_cq(pair + 1)
-
-            rot_bank = qr_banks.tile([P, PAIR, 2, P], F32, tag="bank")
-            for s in range(PAIR):
-                mx_pass(nc, rot_bank[:, s, :, :].rearrange("p e m -> p (e m)"), columns(cq_mx[pair], s * P, P), wqr_mx)
-            by_cos = rope_pool.tile([P, PAIR, 2, P], F32, tag="by_cos")
-            nc.vector.tensor_tensor(
-                out=by_cos[:],
-                in0=rot_bank[:],
-                in1=cos_table[:, a : a + PAIR, :].unsqueeze(2).to_broadcast([P, PAIR, 2, P]),
-                op=MULT,
-            )
             if pair + 2 < N_PAIRS:
                 quantise_x(pair + 2)
             if pair + 1 < N_PAIRS:
                 quantise_cq(pair + 1)
-            by_sin = rope_pool.tile([P, PAIR, 2, P], F32, tag="by_sin")
+
+            rot_bank = qr_banks.tile([P, PAIR, 2 * P], F32, tag="bank")
+            for s in range(PAIR):
+                mx_pass(nc, rot_bank[:, s, :], columns(cq_mx[pair], s * P, P), wqr_mx)
+            products = rope_pool.tile([P, PAIR, 2, 2, P], F32, tag="products")
             nc.vector.tensor_tensor(
-                out=by_sin[:, :, 0, :], in0=rot_bank[:, :, 1, :], in1=minus_sin_table[:, a : a + PAIR, :], op=MULT
+                out=products[:].rearrange("p s f e m -> p s f (e m)"),
+                in0=rot_bank[:].unsqueeze(2).to_broadcast([P, PAIR, 2, 2 * P]),
+                in1=rotation[:, a : a + PAIR, :, :, :].rearrange("p s f e m -> p s f (e m)"),
+                op=MULT,
             )
-            nc.vector.tensor_tensor(
-                out=by_sin[:, :, 1, :], in0=rot_bank[:, :, 0, :], in1=sin_table[:, a : a + PAIR, :], op=MULT
-            )
+            q_r_rows = rows_pool.tile([P, PAIR, ROT], F32, tag="q_r")
             nc.gpsimd.tensor_tensor(
-                out=q_r_rows[:, first : first + PAIR, :].rearrange("p s (m e) -> p s m e", e=2),
-                in0=by_cos[:].rearrange("p s e m -> p s m e"),
-                in1=by_sin[:].rearrange("p s e m -> p s m e"),
+                out=q_r_rows[:].rearrange("p s (m f) -> p s m f", f=2),
+                in0=products[:, :, :, 0, :].rearrange("p s f m -> p s m f"),
+                in1=products[:, :, :, 1, :].rearrange("p s f m -> p s m f"),
                 op=ADD,
             )
 
             for h in range(NH):
+                q_abs_rows = rows_pool.tile([P, PAIR, NLKV], F32, tag="q_abs")
+                copy = nc.vector.tensor_copy if last and h == 1 else nc.scalar.copy
                 for s in range(PAIR):
                     acc = qa_banks.tile([P, NLKV], F32, tag="bank")
                     mx_pass(nc, acc[:], columns(cq_mx[pair], s * P, P), columns(keff_mx, h * NLKV, NLKV))
-                    nc.scalar.copy(out=q_abs_rows[h][:, first + s, :], in_=acc[:])
-                if last_of_group:
-                    nc.sync.dma_start(out=q_abs_view[b, h, :, group_tiles, :], in_=q_abs_rows[h][:])
-                    if h == 0:
-                        nc.sync.dma_start(out=q_r_view[b, :, group_tiles, :], in_=q_r_rows[:])
+                    copy(out=q_abs_rows[:, s, :], in_=acc[:])
+                nc.sync.dma_start(out=q_abs_view[b, h, :, a : a + PAIR, :], in_=q_abs_rows[:])
+                if h == 0:
+                    nc.sync.dma_start(out=q_r_view[b, :, a : a + PAIR, :], in_=q_r_rows[:])

@@ -60,7 +60,7 @@ def tile_causalselfattention_pa_t_kernel(tc, x, cos, sin, W_dq, W_uq, W_uk, W_qr
         const = ctx.enter_context(tc.tile_pool(name="const", bufs=1))
         grouped_pool = ctx.enter_context(tc.tile_pool(name="grouped", bufs=2))
         mx_pool = ctx.enter_context(tc.tile_pool(name="mx", bufs=3))
-        rope_pool = ctx.enter_context(tc.tile_pool(name="rope", bufs=2))
+        rope_pool = ctx.enter_context(tc.tile_pool(name="rope", bufs=3))
         rows_pool = ctx.enter_context(tc.tile_pool(name="rows", bufs=6))
         tr_banks = ctx.enter_context(tc.psum_pool(name="tr_banks", bufs=1))
         cq_banks = ctx.enter_context(tc.psum_pool(name="cq_banks", bufs=2))
@@ -81,35 +81,36 @@ def tile_causalselfattention_pa_t_kernel(tc, x, cos, sin, W_dq, W_uq, W_uk, W_qr
             nc.sync.dma_start(out=x_rows[:], in_=x_view[b, :, part * GROUP : (part + 1) * GROUP, :])
             x_words.append(x_rows[:].bitcast(F32))
 
+        wuq_rows = const.tile([P, PACK, NH * HS], BF16)
+        nc.sync.dma_start(out=wuq_rows[:], in_=W_uq.rearrange("(m j) c -> m j c", j=PACK))
+        trig = const.tile([P, 3, TILES_PER_BATCH, DHR // 2], BF16)
+        nc.sync.dma_start(out=trig[:, 1, :, :], in_=cos.rearrange("(p a) i -> p a i", a=TILES_PER_BATCH))
+        nc.sync.dma_start(out=trig[:, 2, :, :], in_=sin.rearrange("(p a) i -> p a i", a=TILES_PER_BATCH))
         wdq_rows = const.tile([P, PACK, C], BF16)
         nc.sync.dma_start(out=wdq_rows[:], in_=W_dq.rearrange("(m j) k -> m j k", j=PACK))
         load_x(0)
-        wuq_rows = const.tile([P, PACK, NH * HS], BF16)
-        nc.sync.dma_start(out=wuq_rows[:], in_=W_uq.rearrange("(m j) c -> m j c", j=PACK))
         wuk_rows = const.tile([P, NH, WORDS, NLKV], BF16)
         nc.sync.dma_start(out=wuk_rows[:], in_=W_uk.rearrange("(h q e) n -> q h e n", h=NH, e=WORDS))
         wqr_rows = const.tile([P, 2, NLQ], BF16)
         nc.sync.dma_start(out=wqr_rows[:], in_=W_qr.rearrange("(m e) l -> m e l", e=2))
-        cos_rows = const.tile([P, TILES_PER_BATCH, DHR // 2], BF16)
-        nc.sync.dma_start(out=cos_rows[:], in_=cos.rearrange("(p a) i -> p a i", a=TILES_PER_BATCH))
-        sin_rows = const.tile([P, TILES_PER_BATCH, DHR // 2], BF16)
-        nc.sync.dma_start(out=sin_rows[:], in_=sin.rearrange("(p a) i -> p a i", a=TILES_PER_BATCH))
         for group in range(1, N_GROUPS):
             load_x(group)
 
         identity = const.tile([P, P], F32)
         make_identity(nc, identity[:])
 
-        rotation = const.tile([P, TILES_PER_BATCH, 2, 2, P], F32)
-        for f, e, rows, sign in ((0, 0, cos_rows, 1.0), (0, 1, sin_rows, -1.0), (1, 0, sin_rows, 1.0), (1, 1, cos_rows, 1.0)):
-            nc.gpsimd.tensor_scalar(
-                out=rotation[:, :, f, e, :].rearrange("p a (h i) -> p a h i", h=NH),
-                in0=rows[:].unsqueeze(2).to_broadcast([P, TILES_PER_BATCH, NH, DHR // 2]),
-                scalar1=sign,
-                scalar2=0.0,
-                op0=MULT,
-                op1=ADD,
-            )
+        def times(out, in0, factor):
+            nc.gpsimd.tensor_scalar(out=out, in0=in0, scalar1=factor, scalar2=0.0, op0=MULT, op1=ADD)
+
+        times(trig[:, 0, :, :], trig[:, 2, :, :], -1.0)
+        rotation = const.tile([P, TILES_PER_BATCH, 2, P, 2], F32)
+        for e in range(2):
+            for h in range(NH):
+                times(
+                    rotation[:, :, e, h * (DHR // 2) : (h + 1) * (DHR // 2), :],
+                    trig[:, 1 - e : 3 - e, :, :].rearrange("p f a i -> p a i f"),
+                    1.0,
+                )
 
         def transpose_two_tiles(bank, tiles_of_words):
             for s, words in enumerate(tiles_of_words):
@@ -118,6 +119,16 @@ def tile_causalselfattention_pa_t_kernel(tc, x, cos, sin, W_dq, W_uq, W_uk, W_qr
 
         def regroup_words(copy, grouped, bank):
             copy(out=grouped.bitcast(F32), in_=bank[:].rearrange("p u c -> p c u"))
+
+        wuq_words = wuq_rows[:].bitcast(F32)
+        wuq_t = []
+        for h, copy in enumerate((nc.scalar.copy, nc.vector.tensor_copy)):
+            bank = qa_banks.tile([P, PACK, P], F32, tag="bank")
+            for j in range(PACK):
+                nc.tensor.transpose(bank[:, j, :], wuq_words[:, j, h * P : (h + 1) * P], identity[:])
+            transposed = const.tile([P, PACK * P], F32, name="wuq_t%d" % h)
+            copy(out=transposed[:], in_=bank[:].rearrange("p j m -> p (j m)"))
+            wuq_t.append(transposed[:].bitcast(BF16).rearrange("p (c e) -> p c e", e=WORDS))
 
         wdq_words = wdq_rows[:].bitcast(F32)
         wdq_grouped = const.tile([P, NLQ, PACK], BF16, align_bytes=64)
@@ -163,34 +174,10 @@ def tile_causalselfattention_pa_t_kernel(tc, x, cos, sin, W_dq, W_uq, W_uk, W_qr
         transpose_x(0)
         quantise_x(0)
 
-        wuq_words = wuq_rows[:].bitcast(F32)
-        wuq_t = []
-        for h, copy in enumerate((nc.scalar.copy, nc.vector.tensor_copy)):
-            bank = qa_banks.tile([P, PACK, P], F32, tag="bank")
-            for j in range(PACK):
-                nc.tensor.transpose(bank[:, j, :], wuq_words[:, j, h * P : (h + 1) * P], identity[:])
-            transposed = const.tile([P, PACK * P], F32, name="wuq_t%d" % h)
-            copy(out=transposed[:], in_=bank[:].rearrange("p j m -> p (j m)"))
-            wuq_t.append(transposed[:].bitcast(BF16).rearrange("p (c e) -> p c e", e=WORDS))
-
-        transpose_x(1)
-        quantise_x(1)
-        project_cq(0)
-
-        wqr_words = wqr_rows[:].bitcast(F32).rearrange("m e (p u) -> m e u p", u=WORDS)
-        wqr_grouped = const.tile([P, ROT, PACK], BF16, align_bytes=64)
-        wqr_mx = mx_tiles(const, ROT, "wqr")
-        bank = qr_banks.tile([P, WORDS, ROT], F32, tag="bank")
-        for e in range(2):
-            for u in range(WORDS):
-                nc.tensor.transpose(bank[:, u, e * P : (e + 1) * P], wqr_words[:, e, u, :], identity[:])
-        regroup_words(nc.scalar.copy, wqr_grouped[:], bank)
-        quantise_cq(0)
-        quantise(nc, wqr_grouped[:], wqr_mx)
-
         keff_grouped = const.tile([P, NH * NLKV, PACK], BF16, align_bytes=64)
         keff_mx = mx_tiles(const, NH * NLKV, "keff")
-        for h in range(NH):
+
+        def make_keff(h):
             for n_block in range(NLKV // P):
                 bank = qa_banks.tile([P, PACK, P], F32, tag="bank")
                 for j in range(PACK):
@@ -207,6 +194,24 @@ def tile_causalselfattention_pa_t_kernel(tc, x, cos, sin, W_dq, W_uq, W_uk, W_qr
                 copy(out=keff_grouped[:, first : first + P, :], in_=bank[:].rearrange("p j n -> p n j"))
             quantise(nc, keff_grouped[:, h * NLKV : (h + 1) * NLKV, :], columns(keff_mx, h * NLKV, NLKV))
 
+        make_keff(0)
+        project_cq(0)
+        transpose_x(1)
+
+        wqr_words = wqr_rows[:].bitcast(F32).rearrange("m e (p u) -> m e u p", u=WORDS)
+        wqr_grouped = const.tile([P, ROT, PACK], BF16, align_bytes=64)
+        wqr_mx = mx_tiles(const, ROT, "wqr")
+        bank = qr_banks.tile([P, WORDS, ROT], F32, tag="bank")
+        for e in range(2):
+            for u in range(WORDS):
+                nc.tensor.transpose(bank[:, u, e * P : (e + 1) * P], wqr_words[:, e, u, :], identity[:])
+        regroup_words(nc.scalar.copy, wqr_grouped[:], bank)
+        quantise_cq(0)
+        quantise_x(1)
+        quantise(nc, wqr_grouped[:], wqr_mx)
+
+        make_keff(1)
+
         q_abs_view = out_0.rearrange("b h (p a) n -> b h p a n", a=TILES_PER_BATCH)
         q_r_view = out_1.rearrange("b (p a) h d -> b p a (h d)", a=TILES_PER_BATCH)
         for pair in range(N_PAIRS):
@@ -217,36 +222,41 @@ def tile_causalselfattention_pa_t_kernel(tc, x, cos, sin, W_dq, W_uq, W_uk, W_qr
                 transpose_x(pair + 2)
             if pair + 1 < N_PAIRS:
                 project_cq(pair + 1)
-            if pair + 2 < N_PAIRS:
-                quantise_x(pair + 2)
-            if pair + 1 < N_PAIRS:
-                quantise_cq(pair + 1)
 
             rot_bank = qr_banks.tile([P, PAIR, 2 * P], F32, tag="bank")
             for s in range(PAIR):
                 mx_pass(nc, rot_bank[:, s, :], columns(cq_mx[pair], s * P, P), wqr_mx)
-            products = rope_pool.tile([P, PAIR, 2, 2, P], F32, tag="products")
-            nc.vector.tensor_tensor(
-                out=products[:].rearrange("p s f e m -> p s f (e m)"),
-                in0=rot_bank[:].unsqueeze(2).to_broadcast([P, PAIR, 2, 2 * P]),
-                in1=rotation[:, a : a + PAIR, :, :, :].rearrange("p s f e m -> p s f (e m)"),
-                op=MULT,
-            )
+
+            products = rope_pool.tile([P, PAIR, 2, P, 2], F32, tag="products")
+
+            def rotate(s):
+                nc.vector.tensor_tensor(
+                    out=products[:, s, :, :, :].rearrange("p e m f -> p (e m) f"),
+                    in0=rot_bank[:, s, :].unsqueeze(2).to_broadcast([P, 2 * P, 2]),
+                    in1=rotation[:, a + s, :, :, :].rearrange("p e m f -> p (e m) f"),
+                    op=MULT,
+                )
+
+            rotate(0)
+            if pair + 2 < N_PAIRS:
+                quantise_x(pair + 2)
+            if pair + 1 < N_PAIRS:
+                quantise_cq(pair + 1)
+            rotate(1)
             q_r_rows = rows_pool.tile([P, PAIR, ROT], F32, tag="q_r")
             nc.gpsimd.tensor_tensor(
-                out=q_r_rows[:].rearrange("p s (m f) -> p s m f", f=2),
-                in0=products[:, :, :, 0, :].rearrange("p s f m -> p s m f"),
-                in1=products[:, :, :, 1, :].rearrange("p s f m -> p s m f"),
+                out=q_r_rows[:],
+                in0=products[:, :, 0, :, :].rearrange("p s m f -> p s (m f)"),
+                in1=products[:, :, 1, :, :].rearrange("p s m f -> p s (m f)"),
                 op=ADD,
             )
 
             for h in range(NH):
                 q_abs_rows = rows_pool.tile([P, PAIR, NLKV], F32, tag="q_abs")
-                copy = nc.vector.tensor_copy if last and h == 1 else nc.scalar.copy
                 for s in range(PAIR):
                     acc = qa_banks.tile([P, NLKV], F32, tag="bank")
                     mx_pass(nc, acc[:], columns(cq_mx[pair], s * P, P), columns(keff_mx, h * NLKV, NLKV))
+                    copy = nc.vector.tensor_copy if last and s == 1 else nc.scalar.copy
                     copy(out=q_abs_rows[:, s, :], in_=acc[:])
                 nc.sync.dma_start(out=q_abs_view[b, h, :, a : a + PAIR, :], in_=q_abs_rows[:])
-                if h == 0:
-                    nc.sync.dma_start(out=q_r_view[b, :, a : a + PAIR, :], in_=q_r_rows[:])
+            nc.sync.dma_start(out=q_r_view[b, :, a : a + PAIR, :], in_=q_r_rows[:])

@@ -237,11 +237,11 @@ def tile_causalselfattention_pa_t_kernel(tc, x, cos, sin, W_dq, W_uq, W_uk, W_qr
                     op=MULT,
                 )
 
-            rotate(0)
             if pair + 2 < N_PAIRS:
                 quantise_x(pair + 2)
             if pair + 1 < N_PAIRS:
                 quantise_cq(pair + 1)
+            rotate(0)
             rotate(1)
             q_r_rows = rows_pool.tile([P, PAIR, ROT], F32, tag="q_r")
             nc.gpsimd.tensor_tensor(

@@ -56,7 +56,6 @@ def mx_pass(nc, out, stationary, moving):
 def tile_causalselfattention_pa_t_kernel(tc, x, cos, sin, W_dq, W_uq, W_uk, W_qr, out_0, out_1):
     nc = tc.nc
     with ExitStack() as ctx:
-        ctx.enter_context(tc.manual_schedule())
         const = ctx.enter_context(tc.tile_pool(name="const", bufs=1))
         grouped_pool = ctx.enter_context(tc.tile_pool(name="grouped", bufs=2))
         mx_pool = ctx.enter_context(tc.tile_pool(name="mx", bufs=3))
@@ -237,11 +236,11 @@ def tile_causalselfattention_pa_t_kernel(tc, x, cos, sin, W_dq, W_uq, W_uk, W_qr
                     op=MULT,
                 )
 
+            rotate(0)
             if pair + 2 < N_PAIRS:
                 quantise_x(pair + 2)
             if pair + 1 < N_PAIRS:
                 quantise_cq(pair + 1)
-            rotate(0)
             rotate(1)
             q_r_rows = rows_pool.tile([P, PAIR, ROT], F32, tag="q_r")
             nc.gpsimd.tensor_tensor(

from contextlib import ExitStack

import concourse.mybir as mybir
from concourse.masks import make_identity

F32 = mybir.dt.float32
BF16 = mybir.dt.bfloat16
U32 = mybir.dt.uint32
U8 = mybir.dt.uint8
FP8X4 = mybir.dt.float8_e4m3fn_x4
MULT = mybir.AluOpType.mult
ADD = mybir.AluOpType.add

B, T, C = 4, 1024, 512
NH, HS = 2, 256
NLQ, NLKV, DHR = 512, 512, 128

P = 128
PACK = 4
WORDS = 2
ROT = NH * DHR
TILES_PER_BATCH = T // P
PAIR = 2
GROUP = 4
N_PAIRS = B * TILES_PER_BATCH // PAIR
N_GROUPS = B * TILES_PER_BATCH // GROUP
GROUPS_PER_BATCH = TILES_PER_BATCH // GROUP

FLOPS = 2 * B * T * NLQ * (C + NH * NLKV + ROT) + 2 * NH * NLQ * HS * NLKV


def quantise(nc, grouped, operand):
    codes, scales = operand
    nc.vector.quantize_mx(
        out=codes.bitcast(FP8X4), scales=scales, in_=grouped.rearrange("p c t -> p (c t)")
    )


def columns(operand, first, count):
    codes, scales = operand
    return codes[:, first : first + count], scales[:, first : first + count]


def mx_pass(nc, out, stationary, moving):
    nc.tensor.matmul_mx(
        out=out,
        lhsT=stationary[0].bitcast(FP8X4),
        lhsT_scale=stationary[1],
        rhs=moving[0].bitcast(FP8X4),
        rhs_scale=moving[1],
        start=True,
        stop=True,
    )


def tile_causalselfattention_pa_t_kernel(tc, x, cos, sin, W_dq, W_uq, W_uk, W_qr, out_0, out_1):
    nc = tc.nc
    with ExitStack() as ctx:
        const = ctx.enter_context(tc.tile_pool(name="const", bufs=1))
        grouped_pool = ctx.enter_context(tc.tile_pool(name="grouped", bufs=2))
        mx_pool = ctx.enter_context(tc.tile_pool(name="mx", bufs=3))
        rope_pool = ctx.enter_context(tc.tile_pool(name="rope", bufs=3))
        rows_pool = ctx.enter_context(tc.tile_pool(name="rows", bufs=6))
        tr_banks = ctx.enter_context(tc.psum_pool(name="tr_banks", bufs=1))
        cq_banks = ctx.enter_context(tc.psum_pool(name="cq_banks", bufs=2))
        qa_banks = ctx.enter_context(tc.psum_pool(name="qa_banks", bufs=4))
        qr_banks = ctx.enter_context(tc.psum_pool(name="qr_banks", bufs=1))

        def mx_tiles(pool, width, name):
            codes = pool.tile([P, width], U32, name=name + "_codes", tag=name + "_codes", align_bytes=64)
            scales = pool.tile([P, width], U8, name=name + "_scales", tag=name + "_scales", align_bytes=64)
            return codes[:], scales[:]

        x_view = x.rearrange("b (p a) k -> b p a k", a=TILES_PER_BATCH)
        x_words = []

        def load_x(group):
            b, part = divmod(group, GROUPS_PER_BATCH)
            x_rows = const.tile([P, GROUP, C], BF16, name="x_rows%d" % group)
            nc.sync.dma_start(out=x_rows[:], in_=x_view[b, :, part * GROUP : (part + 1) * GROUP, :])
            x_words.append(x_rows[:].bitcast(F32))

        wuq_rows = const.tile([P, PACK, NH * HS], BF16)
        nc.sync.dma_start(out=wuq_rows[:], in_=W_uq.rearrange("(m j) c -> m j c", j=PACK))
        trig = const.tile([P, 3, TILES_PER_BATCH, DHR // 2], BF16)
        nc.sync.dma_start(out=trig[:, 1, :, :], in_=cos.rearrange("(p a) i -> p a i", a=TILES_PER_BATCH))
        nc.sync.dma_start(out=trig[:, 2, :, :], in_=sin.rearrange("(p a) i -> p a i", a=TILES_PER_BATCH))
        wdq_rows = const.tile([P, PACK, C], BF16)
        nc.sync.dma_start(out=wdq_rows[:], in_=W_dq.rearrange("(m j) k -> m j k", j=PACK))
        load_x(0)
        wuk_rows = const.tile([P, NH, WORDS, NLKV], BF16)
        nc.sync.dma_start(out=wuk_rows[:], in_=W_uk.rearrange("(h q e) n -> q h e n", h=NH, e=WORDS))
        wqr_rows = const.tile([P, 2, NLQ], BF16)
        nc.sync.dma_start(out=wqr_rows[:], in_=W_qr.rearrange("(m e) l -> m e l", e=2))
        for group in range(1, N_GROUPS):
            load_x(group)

        identity = const.tile([P, P], F32)
        make_identity(nc, identity[:])

        def times(out, in0, factor):
            nc.gpsimd.tensor_scalar(out=out, in0=in0, scalar1=factor, scalar2=0.0, op0=MULT, op1=ADD)

        times(trig[:, 0, :, :], trig[:, 2, :, :], -1.0)
        rotation = const.tile([P, TILES_PER_BATCH, 2, P, 2], F32)
        for e in range(2):
            for h in range(NH):
                times(
                    rotation[:, :, e, h * (DHR // 2) : (h + 1) * (DHR // 2), :],
                    trig[:, 1 - e : 3 - e, :, :].rearrange("p f a i -> p a i f"),
                    1.0,
                )

        def transpose_two_tiles(bank, tiles_of_words):
            for s, words in enumerate(tiles_of_words):
                for u in range(WORDS):
                    nc.tensor.transpose(bank[:, u, s * P : (s + 1) * P], words[:, u * P : (u + 1) * P], identity[:])

        def regroup_words(copy, grouped, bank):
            copy(out=grouped.bitcast(F32), in_=bank[:].rearrange("p u c -> p c u"))

        wuq_words = wuq_rows[:].bitcast(F32)
        wuq_t = []
        for h, copy in enumerate((nc.scalar.copy, nc.vector.tensor_copy)):
            bank = qa_banks.tile([P, PACK, P], F32, tag="bank")
            for j in range(PACK):
                nc.tensor.transpose(bank[:, j, :], wuq_words[:, j, h * P : (h + 1) * P], identity[:])
            transposed = const.tile([P, PACK * P], F32, name="wuq_t%d" % h)
            copy(out=transposed[:], in_=bank[:].rearrange("p j m -> p (j m)"))
            wuq_t.append(transposed[:].bitcast(BF16).rearrange("p (c e) -> p c e", e=WORDS))

        wdq_words = wdq_rows[:].bitcast(F32)
        wdq_grouped = const.tile([P, NLQ, PACK], BF16, align_bytes=64)
        wdq_mx = mx_tiles(const, NLQ, "wdq")
        for half, copy in enumerate((nc.scalar.copy, nc.vector.tensor_copy)):
            bank = qa_banks.tile([P, WORDS, PAIR * P], F32, tag="bank")
            transpose_two_tiles(bank, [wdq_words[:, PAIR * half + s, :] for s in range(PAIR)])
            regroup_words(copy, wdq_grouped[:, PAIR * P * half : PAIR * P * (half + 1), :], bank)
        quantise(nc, wdq_grouped[:], wdq_mx)

        x_mx = {}
        cq_mx = {}
        x_grouped = {}
        cq_grouped = {}

        def transpose_x(pair):
            group, first = divmod(pair * PAIR, GROUP)
            bank = tr_banks.tile([P, WORDS, PAIR * P], F32, tag="bank")
            transpose_two_tiles(bank, [x_words[group][:, first + s, :] for s in range(PAIR)])
            grouped = grouped_pool.tile([P, PAIR * P, PACK], BF16, tag="x", align_bytes=64)
            regroup_words(nc.scalar.copy, grouped[:], bank)
            x_grouped[pair] = grouped

        def quantise_x(pair):
            x_mx[pair] = mx_tiles(mx_pool, PAIR * P, "x")
            quantise(nc, x_grouped[pair][:], x_mx[pair])

        def project_cq(pair):
            grouped = grouped_pool.tile([P, PAIR * P, PACK], BF16, tag="cq", align_bytes=64)
            for s in range(PAIR):
                bank = cq_banks.tile([P, PACK, P], F32, tag="bank")
                for j in range(PACK):
                    mx_pass(nc, bank[:, j, :], columns(wdq_mx, j * P, P), columns(x_mx[pair], s * P, P))
                nc.vector.tensor_copy(
                    out=grouped[:, s * P : (s + 1) * P, :], in_=bank[:].rearrange("p j t -> p t j")
                )
            cq_grouped[pair] = grouped

        def quantise_cq(pair):
            cq_mx[pair] = mx_tiles(mx_pool, PAIR * P, "cq")
            quantise(nc, cq_grouped[pair][:], cq_mx[pair])

        transpose_x(0)
        quantise_x(0)

        keff_grouped = const.tile([P, NH * NLKV, PACK], BF16, align_bytes=64)
        keff_mx = mx_tiles(const, NH * NLKV, "keff")

        def make_keff(h):
            for n_block in range(NLKV // P):
                bank = qa_banks.tile([P, PACK, P], F32, tag="bank")
                for j in range(PACK):
                    for e in range(WORDS):
                        nc.tensor.matmul(
                            out=bank[:, j, :],
                            lhsT=wuq_t[h][:, j * P : (j + 1) * P, e],
                            rhs=wuk_rows[:, h, e, n_block * P : (n_block + 1) * P],
                            start=(e == 0),
                            stop=(e == WORDS - 1),
                        )
                copy = nc.scalar.copy if n_block % 2 == 0 else nc.vector.tensor_copy
                first = h * NLKV + n_block * P
                copy(out=keff_grouped[:, first : first + P, :], in_=bank[:].rearrange("p j n -> p n j"))
            quantise(nc, keff_grouped[:, h * NLKV : (h + 1) * NLKV, :], columns(keff_mx, h * NLKV, NLKV))

        make_keff(0)
        project_cq(0)
        transpose_x(1)

        wqr_words = wqr_rows[:].bitcast(F32).rearrange("m e (p u) -> m e u p", u=WORDS)
        wqr_grouped = const.tile([P, ROT, PACK], BF16, align_bytes=64)
        wqr_mx = mx_tiles(const, ROT, "wqr")
        bank = qr_banks.tile([P, WORDS, ROT], F32, tag="bank")
        for e in range(2):
            for u in range(WORDS):
                nc.tensor.transpose(bank[:, u, e * P : (e + 1) * P], wqr_words[:, e, u, :], identity[:])
        regroup_words(nc.scalar.copy, wqr_grouped[:], bank)
        quantise_cq(0)
        quantise_x(1)
        quantise(nc, wqr_grouped[:], wqr_mx)

        make_keff(1)

        q_abs_view = out_0.rearrange("b h (p a) n -> b h p a n", a=TILES_PER_BATCH)
        q_r_view = out_1.rearrange("b (p a) h d -> b p a (h d)", a=TILES_PER_BATCH)
        for pair in range(N_PAIRS):
            b, a = divmod(pair * PAIR, TILES_PER_BATCH)
            last = pair == N_PAIRS - 1

            if pair + 2 < N_PAIRS:
                transpose_x(pair + 2)
            if pair + 1 < N_PAIRS:
                project_cq(pair + 1)

            rot_bank = qr_banks.tile([P, PAIR, 2 * P], F32, tag="bank")
            for s in range(PAIR):
                mx_pass(nc, rot_bank[:, s, :], columns(cq_mx[pair], s * P, P), wqr_mx)

            products = rope_pool.tile([P, PAIR, 2, P, 2], F32, tag="products")

            def rotate(s):
                nc.vector.tensor_tensor(
                    out=products[:, s, :, :, :].rearrange("p e m f -> p (e m) f"),
                    in0=rot_bank[:, s, :].unsqueeze(2).to_broadcast([P, 2 * P, 2]),
                    in1=rotation[:, a + s, :, :, :].rearrange("p e m f -> p (e m) f"),
                    op=MULT,
                )

            rotate(0)
            if pair + 2 < N_PAIRS:
                quantise_x(pair + 2)
            if pair + 1 < N_PAIRS:
                quantise_cq(pair + 1)
            rotate(1)
            q_r_rows = rows_pool.tile([P, PAIR, ROT], F32, tag="q_r")
            nc.gpsimd.tensor_tensor(
                out=q_r_rows[:],
                in0=products[:, :, 0, :, :].rearrange("p s m f -> p s (m f)"),
                in1=products[:, :, 1, :, :].rearrange("p s m f -> p s (m f)"),
                op=ADD,
            )

            for h in range(NH):
                q_abs_rows = rows_pool.tile([P, PAIR, NLKV], F32, tag="q_abs")
                for s in range(PAIR):
                    acc = qa_banks.tile([P, NLKV], F32, tag="bank")
                    mx_pass(nc, acc[:], columns(cq_mx[pair], s * P, P), columns(keff_mx, h * NLKV, NLKV))
                    copy = nc.vector.tensor_copy if last and s == 1 else nc.scalar.copy
                    copy(out=q_abs_rows[:, s, :], in_=acc[:])
                nc.sync.dma_start(out=q_abs_view[b, h, :, a : a + PAIR, :], in_=q_abs_rows[:])
            nc.sync.dma_start(out=q_r_view[b, :, a : a + PAIR, :], in_=q_r_rows[:])
